import numpy as np
import ml_dtypes


def mxq(x, axis, fmt="e4m3"):
    dtype, down = {"e4m3": (ml_dtypes.float8_e4m3fn, 7), "e5m2": (ml_dtypes.float8_e5m2, 14)}[fmt]
    v = np.moveaxis(np.asarray(x, np.float32).astype(ml_dtypes.bfloat16).astype(np.float64), axis, -1)
    blocks = v.reshape(v.shape[:-1] + (-1, 32))
    amax = np.abs(blocks).max(-1, keepdims=True)
    byte = np.maximum(np.where(amax > 0, np.frexp(amax)[1] - 1 + 127, 0) - down, 1)
    scale = np.exp2(byte - 127.0)
    codes = (blocks / scale).astype(np.float32).astype(dtype).astype(np.float64)
    return np.moveaxis((codes * scale).reshape(v.shape), -1, axis)


WIDE = False


def mx_kscale(k):
    if not WIDE:
        return np.ones(k)
    levels = np.array([18, -18])
    if k % 512:
        return np.exp2(np.random.permutation(np.resize(levels, k // 32))).repeat(32)
    a = np.empty((k // 512, 16))
    for p in range(k // 512):
        a[p, :8] = np.random.permutation(np.resize(levels, 8))
        for g in range(8):
            far = levels[np.abs(levels - a[p, g]) >= 10]
            a[p, g + 8] = far[np.random.randint(len(far))]
    return np.exp2(a.ravel()).repeat(32)


BF16 = ml_dtypes.bfloat16


def bf(x):
    return np.asarray(x, np.float32).astype(BF16)


def f64(x):
    return np.asarray(x).astype(np.float64)


B, IN, G, OUT = 1024, 512, 8, 512
K = IN * G
GRID_MIN, GRID_MAX = -2.0, 2.0
H = (GRID_MAX - GRID_MIN) / (G - 1)


def setup_inputs():
    s = mx_kscale(B)
    u = mx_kscale(OUT)
    a = np.log2(s.max() / s)[:, None]
    grid = bf(np.linspace(GRID_MIN, GRID_MAX, G) + 0.02 * np.random.standard_normal(G))
    z = np.random.standard_normal((B, IN))
    even = np.arange(IN) % 2 == 0
    side = np.where(even, 1.0, -1.0)
    edge = np.where(even, f64(grid).max(), f64(grid).min())
    far = edge + side * H * np.sqrt(a * np.log(2.0)) + 0.05 * z
    x = np.where(a > 0, far, z)
    w = np.random.standard_normal((K, OUT)) / np.sqrt(IN) / u
    g = np.random.standard_normal((B, OUT)) * np.exp2(np.random.randint(-6, 1, (B, 1))) * np.exp2(a) * u
    return {"x": bf(x), "grid": grid, "spline_weight": bf(w), "grad_out": bf(g)}


def reference(x, grid, spline_weight, grad_out):
    h = (GRID_MAX - GRID_MIN) / (G - 1)
    g = f64(grad_out)
    d = f64(x)[..., None] - f64(grid)
    basis = np.exp(-np.square(d / h))
    dbasis = mxq(g, 1, "e5m2") @ mxq(f64(spline_weight), 1, "e4m3").T
    dx = (dbasis.reshape(d.shape) * basis * (-2.0 * d / (h * h))).sum(axis=-1)
    dw = mxq(basis.reshape(basis.shape[0], -1), 0, "e4m3").T @ mxq(g, 0, "e5m2")
    return dx, dw

@@ -1,0 +1,401 @@
+from contextlib import ExitStack
+
+import concourse.mybir as mybir
+from concourse.masks import make_identity
+
+F32 = mybir.dt.float32
+BF16 = mybir.dt.bfloat16
+U32 = mybir.dt.uint32
+U8 = mybir.dt.uint8
+E4M3 = mybir.dt.float8_e4m3fn_x4
+E5M2 = mybir.dt.float8_e5m2_x4
+ACT = mybir.ActivationFunctionType
+ALU = mybir.AluOpType
+
+B, IN, G, OUT = 1024, 512, 8, 512
+FLOPS = 2 * 2 * B * IN * G * OUT
+P = 128
+INV_H = 1.75
+OUT_SCALE = -2.0 * INV_H * INV_H
+UNITS = 16
+REF = 3
+BSET = ()
+VSET = ()
+
+
+def tile_gaussiankernel_v_kernel(tc, x, grid, spline_weight, grad_out, out_0, out_1):
+    nc = tc.nc
+    x_v = x.rearrange("(g p t) i -> g p t i", g=2, t=4)
+    go_v = grad_out.rearrange("(g p t) o -> g p t o", g=2, t=4)
+    w_v = spline_weight.rearrange("(q p j) o -> q p j o", q=4, j=8)
+    o0_v = out_0.rearrange("(g p t) i -> g p t i", g=2, t=4)
+    o1_v = out_1.rearrange("(q p j) o -> q p j o", q=4, j=8)
+
+    with ExitStack() as ctx:
+        keep = ctx.enter_context(tc.tile_pool(name="keep", bufs=1))
+        work = ctx.enter_context(tc.tile_pool(name="work", bufs=2))
+        ps = ctx.enter_context(tc.psum_pool(name="ps", bufs=1))
+
+        ident = keep.tile([P, P], F32, name="ident")
+        grid_bf = keep.tile([P, G], BF16, name="grid_bf")
+        grid_f = keep.tile([P, G], F32, name="grid_f")
+        grid_n = keep.tile([P, G], F32, name="grid_n")
+        grid_d = keep.tile([P, G], F32, name="grid_d")
+        ident_b = keep.tile([P, P], BF16, name="ident_b")
+        xt_sb = [keep.tile([P, 2, 512], BF16, name="xt%d" % q) for q in range(4)]
+        warm = keep.tile([P, 1], F32, name="warm")
+        x_sb = [keep.tile([P, 4, IN], BF16, name="x%d" % g) for g in range(2)]
+        go_sb = [keep.tile([P, 4, OUT], BF16, name="go%d" % g, align_bytes=64) for g in range(2)]
+        w_sb = [[keep.tile([P, 4, OUT], BF16, name="w%d_%d" % (q, h), align_bytes=64) for h in range(2)] for q in range(4)]
+        gob_i = [keep.tile([P, OUT, 4], BF16, name="gobi%d" % g, align_bytes=64) for g in range(2)]
+        gob_c = [keep.tile([P, OUT], U32, name="gobc%d" % g, align_bytes=64) for g in range(2)]
+        gob_s = [keep.tile([P, OUT], U8, name="gobs%d" % g, align_bytes=64) for g in range(2)]
+        got_i = {}
+        got_c = [keep.tile([P, 512], U32, name="gotc%d" % g, align_bytes=64) for g in range(2)]
+        got_s = [keep.tile([P, 512], U8, name="gots%d" % g, align_bytes=64) for g in range(2)]
+        w_c = [[keep.tile([P, 512], U32, name="wc%d_%d" % (q, h), align_bytes=64) for h in range(2)] for q in range(4)]
+        w_s = [[keep.tile([P, 512], U8, name="ws%d_%d" % (q, h), align_bytes=64) for h in range(2)] for q in range(4)]
+
+        E = {}
+        PP = {}
+        GP = {}
+        T1 = {}
+        Y0 = {}
+        Y1 = {}
+        EB = {}
+        EC = {}
+        ES = {}
+        WI = {}
+        DT = {}
+        TB = {}
+        BK = {}
+        OP = {}
+        OS = {}
+
+        def unit(u):
+            return u // 4, (u // 2) % 2, u % 2
+
+        def sq(u, jj):
+            q, g, h = unit(u)
+            if jj == 0:
+                E[u] = work.tile([P, 4, 4, P], F32, name="e", bufs=4)
+            j = 4 * h + jj
+            nc.scalar.activation(
+                out=E[u][:, :, jj, :], in_=x_sb[g][:, :, q * P : (q + 1) * P],
+                func=ACT.Square, scale=INV_H, bias=grid_n[:, j : j + 1],
+            )
+
+        def exp(u):
+            flat = E[u][:].rearrange("p t j i -> p (t j i)")
+            nc.scalar.activation(out=flat, in_=flat, func=ACT.Exp, scale=-1.0)
+
+        def cast(u):
+            EB[u] = work.tile([P, 2048], BF16, name="eb", bufs=2, align_bytes=64)
+            nc.vector.tensor_copy(
+                out=EB[u][:].rearrange("p (c i t) -> p c t i", i=4, t=4),
+                in_=E[u][:].rearrange("p t j (c i) -> p (j c) t i", i=4),
+            )
+
+        def fmul(u):
+            q, g, h = unit(u)
+            for jj in range(4):
+                j = 4 * h + jj
+                if j in BSET:
+                    e = E[u][:, :, jj, :]
+                    nc.vector.scalar_tensor_tensor(
+                        out=e, in0=x_sb[g][:, :, q * P : (q + 1) * P], scalar=grid_f[:, j : j + 1], in1=e,
+                        op0=ALU.subtract, op1=ALU.mult,
+                    )
+
+        def quant(u):
+            EC[u] = work.tile([P, 512], U32, name="ec", bufs=7, align_bytes=64)
+            ES[u] = work.tile([P, 512], U8, name="es", bufs=7, align_bytes=64)
+            nc.vector.quantize_mx(out=EC[u][:].bitcast(E4M3), scales=ES[u][:], in_=EB[u][:])
+
+        def dmm(u, t):
+            q, g, h = unit(u)
+            DT[u, t] = ps.tile([P, 512], F32, name="d", bufs=3)
+            c = slice(t * P, (t + 1) * P)
+            nc.tensor.matmul_mx(
+                out=DT[u, t][:], lhsT=got_c[g][:, c].bitcast(E5M2), lhsT_scale=got_s[g][:, c],
+                rhs=w_c[q][h][:].bitcast(E4M3), rhs_scale=w_s[q][h][:], start=True, stop=True,
+            )
+
+        def pmul(u, t):
+            if t == 0:
+                PP[u] = work.tile([P, 4, 4, P], F32, name="pp", bufs=3)
+            nc.vector.tensor_tensor(
+                out=PP[u][:, t].rearrange("p j i -> p (j i)"), in0=DT[u, t][:],
+                in1=E[u][:, t].rearrange("p j i -> p (j i)"), op=ALU.mult,
+            )
+
+        def gscale(u, eng):
+            h = u % 2
+            GP[u] = work.tile([P, 4, 4, P], F32, name="gp", bufs=2)
+            for jj in range(4):
+                j = 4 * h + jj
+                if j != REF and j not in BSET:
+                    (nc.vector if j in VSET else eng).tensor_scalar(
+                        out=GP[u][:, :, jj, :], in0=PP[u][:, :, jj, :], scalar1=grid_d[:, j : j + 1], scalar2=0.0,
+                        op0=ALU.mult, op1=ALU.add,
+                    )
+
+        def addt(out, src, first, last):
+            nc.tensor.matmul(out, lhsT=src, rhs=ident[:], start=first, stop=last, is_transpose=True)
+
+        def tsum0(u):
+            s, h = u // 2, u % 2
+            if h == 0:
+                TB[s] = ps.tile([P, 512], F32, name="t0", bufs=1)
+            js = [j for j in range(4 * h, 4 * h + 4) if j not in BSET]
+            for t in range(4):
+                for j in js:
+                    addt(
+                        TB[s][:, t * P : (t + 1) * P], PP[u][:, t, j % 4, :], h == 0 and t == 0 and j == js[0],
+                        h == 1 and t == 3 and j == js[-1],
+                    )
+
+        def tsum1(u):
+            s, h = u // 2, u % 2
+            if h == 0:
+                T1[s] = ps.tile([P, 512], F32, name="t1", bufs=1)
+            js = [j for j in range(4 * h, 4 * h + 4) if j != REF]
+            for t in range(4):
+                for j in js:
+                    src = PP[u] if j in BSET else GP[u]
+                    addt(
+                        T1[s][:, t * P : (t + 1) * P], src[:, t, j % 4, :], h == 0 and t == 0 and j == js[0],
+                        h == 1 and t == 3 and j == js[-1],
+                    )
+
+        def xtrans(q):
+            bank = ps.tile([P, 2, 4, P], BF16, name="m", bufs=3)
+            for g in range(2):
+                for t in range(4):
+                    nc.tensor.transpose(bank[:, g, t, :], x_sb[g][:, t, q * P : (q + 1) * P], ident_b[:])
+            return bank
+
+        def xevac(q, bank):
+            nc.scalar.copy(out=xt_sb[q][:].rearrange("p g c -> p (g c)"), in_=bank[:].rearrange("p g t c -> p (g t c)"))
+
+        def y0evac(s):
+            Y0[s] = work.tile([P, 512], F32, name="y0", bufs=2)
+            nc.vector.scalar_tensor_tensor(
+                out=Y0[s][:], in0=xt_sb[s // 2][:, s % 2, :], scalar=grid_f[:, REF : REF + 1], in1=TB[s][:],
+                op0=ALU.subtract, op1=ALU.mult,
+            )
+
+        def y1evac(s):
+            Y1[s] = work.tile([P, 512], F32, name="y1", bufs=2)
+            nc.scalar.copy(out=Y1[s][:], in_=T1[s][:])
+
+        def back(s):
+            BK[s] = ps.tile([P, 512], F32, name="m", bufs=3)
+            for k, y in ((0, Y0[s]), (1, Y1[s])):
+                for t in range(4):
+                    c = slice(t * P, (t + 1) * P)
+                    addt(BK[s][:, c], y[:, c], k == 0 and t == 0, k == 1 and t == 3)
+
+        def backevac(s):
+            q, g = s // 2, s % 2
+            o = work.tile([P, 4, P], F32, name="o0", bufs=3)
+            nc.scalar.activation(out=o[:].rearrange("p t i -> p (t i)"), in_=BK[s][:], func=ACT.Copy, scale=OUT_SCALE)
+            nc.sync.dma_start(out=o0_v[g][:, :, q * P : (q + 1) * P], in_=o[:])
+
+        def omm(q, j):
+            OP[q, j] = ps.tile([P, 512], F32, name="m", bufs=3)
+            h, jj = j // 4, j % 4
+            c = slice(jj * P, (jj + 1) * P)
+            for g in range(2):
+                u = 4 * q + 2 * g + h
+                nc.tensor.matmul_mx(
+                    out=OP[q, j][:], lhsT=EC[u][:, c].bitcast(E4M3), lhsT_scale=ES[u][:, c],
+                    rhs=gob_c[g][:].bitcast(E5M2), rhs_scale=gob_s[g][:], start=(g == 0), stop=(g == 1),
+                )
+
+        def oevac(q, j, eng="s"):
+            if j % 2 == 0:
+                OS[q, j // 2] = work.tile([P, 2, 512], F32, name="os", bufs=3)
+            st = OS[q, j // 2]
+            if eng == "s":
+                nc.scalar.copy(out=st[:, j % 2, :], in_=OP[q, j][:])
+            else:
+                nc.vector.tensor_copy(out=st[:, j % 2, :], in_=OP[q, j][:])
+            if j % 2 == 1:
+                nc.sync.dma_start(out=o1_v[q][:, j - 1 : j + 1, :], in_=st[:])
+
+        def words(src2d, bank, half):
+            w = src2d.bitcast(F32)
+            for r in range(2):
+                nc.tensor.transpose(bank[:, half, r, :], w[:, r : 256 : 2], ident[:])
+
+        def wtrans(q, h, k):
+            bank = ps.tile([P, 2, 2, P], F32, name="m", bufs=3)
+            for a in range(2):
+                words(w_sb[q][h][:, 2 * k + a, :], bank, a)
+            return bank
+
+        def spread(eng, dst, k, bank):
+            o = dst.bitcast(F32)[:, k * 512 : (k + 1) * 512].rearrange("p (a r e) -> p a r e", a=2, e=2)
+            i = bank[:].rearrange("p a e r -> p a r e")
+            if eng == "s":
+                nc.scalar.copy(out=o, in_=i)
+            else:
+                nc.vector.tensor_copy(out=o, in_=i)
+
+        def wtile(q, h):
+            WI[q, h] = work.tile([P, 2048], BF16, name="wi", bufs=3, align_bytes=64)
+
+        def wquant(q, h):
+            nc.vector.quantize_mx(out=w_c[q][h][:].bitcast(E4M3), scales=w_s[q][h][:], in_=WI[q, h][:])
+
+        def gtrans(g, k):
+            bank = ps.tile([P, 2, 2, P], F32, name="m", bufs=3)
+            for a in range(2):
+                words(go_sb[g][:, 2 * k + a, :], bank, a)
+            return bank
+
+        def gtquant(g):
+            nc.vector.quantize_mx(out=got_c[g][:].bitcast(E5M2), scales=got_s[g][:], in_=got_i[g][:])
+
+        def gbquant(g):
+            nc.vector.quantize_mx(
+                out=gob_c[g][:].bitcast(E5M2), scales=gob_s[g][:], in_=gob_i[g][:].rearrange("p o t -> p (o t)")
+            )
+
+        def ginter(g, part):
+            c = slice(part * 256, (part + 1) * 256)
+            nc.gpsimd.tensor_scalar(
+                out=gob_i[g][:, c, :].rearrange("p (c i) t -> p c t i", i=4),
+                in0=go_sb[g][:, :, c].rearrange("p t (c i) -> p c t i", i=4),
+                scalar1=1.0, scalar2=0.0, op0=ALU.mult, op1=ALU.add,
+            )
+
+        with tc.manual_schedule():
+            nc.gpsimd.memset(warm[:], 0.0)
+            nc.scalar.dma_start(out=grid_bf[:], in_=grid.partition_broadcast(P))
+            nc.scalar.activation(out=warm[:], in_=warm[:], func=ACT.Exp)
+            nc.sync.dma_start(out=x_sb[0][:], in_=x_v[0])
+            nc.sync.dma_start(out=go_sb[0][:], in_=go_v[0])
+            nc.sync.dma_start(out=w_sb[0][0][:], in_=w_v[0][:, 0:4, :])
+            nc.sync.dma_start(out=w_sb[0][1][:], in_=w_v[0][:, 4:8, :])
+            nc.sync.dma_start(out=go_sb[1][:], in_=go_v[1])
+            nc.sync.dma_start(out=x_sb[1][:], in_=x_v[1])
+            for q in range(1, 4):
+                for h in range(2):
+                    nc.sync.dma_start(out=w_sb[q][h][:], in_=w_v[q][:, 4 * h : 4 * h + 4, :])
+            make_identity(nc, ident[:])
+            make_identity(nc, ident_b[:])
+            nc.vector.tensor_scalar(out=grid_n[:], in0=grid_bf[:], scalar1=-INV_H, scalar2=None, op0=ALU.mult)
+            nc.vector.tensor_copy(out=grid_f[:], in_=grid_bf[:])
+            nc.vector.tensor_scalar(
+                out=grid_d[:], in0=grid_f[:], scalar1=grid_f[:, REF : REF + 1], scalar2=-1.0, op0=ALU.subtract, op1=ALU.mult
+            )
+
+            for jj in range(4):
+                sq(0, jj)
+            exp(0)
+            got_i[0] = work.tile([P, 2048], BF16, name="wi", bufs=3, align_bytes=64)
+            for k in range(2):
+                spread("v", got_i[0][:], k, gtrans(0, k))
+            wtile(0, 0)
+            spread("v", WI[0, 0][:], 0, wtrans(0, 0, 0))
+            gtquant(0)
+            spread("v", WI[0, 0][:], 1, wtrans(0, 0, 1))
+            wtile(0, 1)
+            wbank = [wtrans(0, 1, 0), wtrans(0, 1, 1)]
+            ginter(0, 0)
+            ginter(0, 1)
+            wquant(0, 0)
+            for t in range(3):
+                dmm(0, t)
+            for jj in range(4):
+                sq(1, jj)
+            spread("s", WI[0, 1][:], 0, wbank[0])
+            exp(1)
+
+            o_slots = {}
+            for q in range(4):
+                for j in range(8):
+                    n = 4 * q + 2 + j // 2 if q < 3 else (14 if j < 4 else 15)
+                    o_slots.setdefault(n, []).append((q, j))
+
+            for n in range(UNITS + 3):
+                live = n < UNITS
+                nxt = n + 1 < UNITS
+                todo = o_slots.get(n, [])
+                wq, wh, wk = n // 4 + 1, (n // 2) % 2, n % 2
+                if live:
+                    pmul(n, 0)
+                for q, j in todo[:2]:
+                    omm(q, j)
+                if live:
+                    dmm(n, 3)
+                if n + 2 < UNITS:
+                    sq(n + 2, 0)
+                    sq(n + 2, 1)
+                if live:
+                    pmul(n, 1)
+                    pmul(n, 2)
+                    pmul(n, 3)
+                    gscale(n, nc.gpsimd if n < UNITS - 1 else nc.vector)
+                if n == 0:
+                    cast(0)
+                    spread("v", WI[0, 1][:], 1, wbank[1])
+                    quant(0)
+                    wquant(0, 1)
+                if 1 <= n <= UNITS:
+                    tsum0(n - 1)
+                if 2 <= n <= UNITS + 1:
+                    tsum1(n - 2)
+                if n % 2 == 0 and n >= 4:
+                    back((n - 4) // 2)
+                if n == 0:
+                    got_i[1] = work.tile([P, 2048], BF16, name="wi", bufs=3, align_bytes=64)
+                    spread("v", got_i[1][:], 0, gtrans(1, 0))
+                    spread("v", got_i[1][:], 1, gtrans(1, 1))
+                bank = None
+                if wq < 4:
+                    if wk == 0:
+                        wtile(wq, wh)
+                    bank = wtrans(wq, wh, wk)
+                if n % 4 == 1 and live:
+                    xbank = xtrans(n // 4)
+                if nxt:
+                    for t in range(3):
+                        dmm(n + 1, t)
+                for k, (q, j) in enumerate(todo[:2]):
+                    oevac(q, j, "sv"[k])
+                if n % 4 == 1 and live:
+                    xevac(n // 4, xbank)
+                if n == 0:
+                    ginter(1, 0)
+                    ginter(1, 1)
+                if nxt:
+                    cast(n + 1)
+                    fmul(n + 1)
+                if n + 2 < UNITS:
+                    sq(n + 2, 2)
+                    sq(n + 2, 3)
+                if bank is not None:
+                    spread("sv"[wk], WI[wq, wh][:], wk, bank)
+                if n % 2 == 0 and 2 <= n <= UNITS:
+                    y0evac((n - 2) // 2)
+                if n % 2 == 1 and 3 <= n:
+                    y1evac((n - 3) // 2)
+                if n % 2 == 0 and n >= 4:
+                    backevac((n - 4) // 2)
+                if n + 2 < UNITS:
+                    exp(n + 2)
+                if n == 0:
+                    gtquant(1)
+                if n == 1:
+                    gbquant(0)
+                    gbquant(1)
+                if nxt:
+                    quant(n + 1)
+                if wq < 4 and wk == 1:
+                    wquant(wq, wh)
+                for q, j in todo[2:]:
+                    omm(q, j)
+                    oevac(q, j)

@@ -12,390 +12,462 @@ E5M2 = mybir.dt.float8_e5m2_x4
 ACT = mybir.ActivationFunctionType
 ALU = mybir.AluOpType
 
-B, IN, G, OUT = 1024, 512, 8, 512
-FLOPS = 2 * 2 * B * IN * G * OUT
+TOKENS, INPUTS, GRID, FEATURES = 1024, 512, 8, 512
+FLOPS = 2 * 2 * TOKENS * INPUTS * GRID * FEATURES
+
 P = 128
-INV_H = 1.75
-OUT_SCALE = -2.0 * INV_H * INV_H
+T = 4
+J = 4
+BANK = 512
 UNITS = 16
+BLOCKS = 4
+INV_H = 7.0 / 4.0
+OUT_SCALE = -2.0 * INV_H * INV_H
 REF = 3
-BSET = ()
-VSET = ()
 
 
 def tile_gaussiankernel_v_kernel(tc, x, grid, spline_weight, grad_out, out_0, out_1):
     nc = tc.nc
-    x_v = x.rearrange("(g p t) i -> g p t i", g=2, t=4)
-    go_v = grad_out.rearrange("(g p t) o -> g p t o", g=2, t=4)
-    w_v = spline_weight.rearrange("(q p j) o -> q p j o", q=4, j=8)
-    o0_v = out_0.rearrange("(g p t) i -> g p t i", g=2, t=4)
-    o1_v = out_1.rearrange("(q p j) o -> q p j o", q=4, j=8)
+
+    x_hbm = x.rearrange("(g p t) i -> g p t i", g=2, t=T)
+    grad_hbm = grad_out.rearrange("(g p t) o -> g p t o", g=2, t=T)
+    weight_hbm = spline_weight.rearrange("(q p j) o -> q p j o", q=BLOCKS, j=GRID)
+    out_0_hbm = out_0.rearrange("(g p t) i -> g p t i", g=2, t=T)
+    out_1_hbm = out_1.rearrange("(q p j) o -> q p j o", q=BLOCKS, j=GRID)
 
     with ExitStack() as ctx:
         keep = ctx.enter_context(tc.tile_pool(name="keep", bufs=1))
         work = ctx.enter_context(tc.tile_pool(name="work", bufs=2))
-        ps = ctx.enter_context(tc.psum_pool(name="ps", bufs=1))
+        psum = ctx.enter_context(tc.psum_pool(name="psum", bufs=1))
 
-        ident = keep.tile([P, P], F32, name="ident")
-        grid_bf = keep.tile([P, G], BF16, name="grid_bf")
-        grid_f = keep.tile([P, G], F32, name="grid_f")
-        grid_n = keep.tile([P, G], F32, name="grid_n")
-        grid_d = keep.tile([P, G], F32, name="grid_d")
-        ident_b = keep.tile([P, P], BF16, name="ident_b")
-        xt_sb = [keep.tile([P, 2, 512], BF16, name="xt%d" % q) for q in range(4)]
-        warm = keep.tile([P, 1], F32, name="warm")
-        x_sb = [keep.tile([P, 4, IN], BF16, name="x%d" % g) for g in range(2)]
-        go_sb = [keep.tile([P, 4, OUT], BF16, name="go%d" % g, align_bytes=64) for g in range(2)]
-        w_sb = [[keep.tile([P, 4, OUT], BF16, name="w%d_%d" % (q, h), align_bytes=64) for h in range(2)] for q in range(4)]
-        gob_i = [keep.tile([P, OUT, 4], BF16, name="gobi%d" % g, align_bytes=64) for g in range(2)]
-        gob_c = [keep.tile([P, OUT], U32, name="gobc%d" % g, align_bytes=64) for g in range(2)]
-        gob_s = [keep.tile([P, OUT], U8, name="gobs%d" % g, align_bytes=64) for g in range(2)]
-        got_i = {}
-        got_c = [keep.tile([P, 512], U32, name="gotc%d" % g, align_bytes=64) for g in range(2)]
-        got_s = [keep.tile([P, 512], U8, name="gots%d" % g, align_bytes=64) for g in range(2)]
-        w_c = [[keep.tile([P, 512], U32, name="wc%d_%d" % (q, h), align_bytes=64) for h in range(2)] for q in range(4)]
-        w_s = [[keep.tile([P, 512], U8, name="ws%d_%d" % (q, h), align_bytes=64) for h in range(2)] for q in range(4)]
+        identity = keep.tile([P, P], F32, name="identity")
+        identity_bf = keep.tile([P, P], BF16, name="identity_bf")
+        grid_bf = keep.tile([P, GRID], BF16, name="grid_bf")
+        grid_f = keep.tile([P, GRID], F32, name="grid_f")
+        grid_bias = keep.tile([P, GRID], F32, name="grid_bias")
+        grid_weight = keep.tile([P, GRID], F32, name="grid_weight")
+        one_column = keep.tile([P, 1], F32, name="one_column")
+        x_sb = [keep.tile([P, T, INPUTS], BF16, name="x%d" % g) for g in range(2)]
+        x_t = [keep.tile([P, 2, BANK], BF16, name="xt%d" % q) for q in range(BLOCKS)]
+        grad_sb = [keep.tile([P, T, FEATURES], BF16, name="grad%d" % g, align_bytes=64) for g in range(2)]
 
-        E = {}
-        PP = {}
-        GP = {}
-        T1 = {}
-        Y0 = {}
-        Y1 = {}
-        EB = {}
-        EC = {}
-        ES = {}
-        WI = {}
-        DT = {}
-        TB = {}
-        BK = {}
-        OP = {}
-        OS = {}
+        tok_in = [keep.tile([P, FEATURES, T], BF16, name="toki%d" % g, align_bytes=64) for g in range(2)]
+        tok_codes = [keep.tile([P, FEATURES], U32, name="tokc%d" % g, align_bytes=64) for g in range(2)]
+        tok_scales = [keep.tile([P, FEATURES], U8, name="toks%d" % g, align_bytes=64) for g in range(2)]
+        feat_codes = [keep.tile([P, BANK], U32, name="featc%d" % g, align_bytes=64) for g in range(2)]
+        feat_scales = [keep.tile([P, BANK], U8, name="feats%d" % g, align_bytes=64) for g in range(2)]
+        w_codes = [keep.tile([P, BANK], U32, name="wc%d" % c, align_bytes=64) for c in range(2 * BLOCKS)]
+        w_scales = [keep.tile([P, BANK], U8, name="ws%d" % c, align_bytes=64) for c in range(2 * BLOCKS)]
+
+        w_raw, paired, banks = {}, {}, {}
+        basis, rounded, codes, scales = {}, {}, {}, {}
+        dbasis, prod, scaled = {}, {}, {}
+        plain_sum, weighted_sum, plain_sb, weighted_sb, result = {}, {}, {}, {}, {}
+        acc, staged = {}, {}
 
         def unit(u):
             return u // 4, (u // 2) % 2, u % 2
 
-        def sq(u, jj):
-            q, g, h = unit(u)
-            if jj == 0:
-                E[u] = work.tile([P, 4, 4, P], F32, name="e", bufs=4)
-            j = 4 * h + jj
-            nc.scalar.activation(
-                out=E[u][:, :, jj, :], in_=x_sb[g][:, :, q * P : (q + 1) * P],
-                func=ACT.Square, scale=INV_H, bias=grid_n[:, j : j + 1],
-            )
 
-        def exp(u):
-            flat = E[u][:].rearrange("p t j i -> p (t j i)")
-            nc.scalar.activation(out=flat, in_=flat, func=ACT.Exp, scale=-1.0)
+        def load_weight(c):
+            w_raw[c] = work.tile([P, J, FEATURES], BF16, name="w_raw", bufs=5, align_bytes=64)
+            first = J * (c % 2)
+            nc.sync.dma_start(out=w_raw[c][:], in_=weight_hbm[c // 2][:, first : first + J, :])
 
-        def cast(u):
-            EB[u] = work.tile([P, 2048], BF16, name="eb", bufs=2, align_bytes=64)
-            nc.vector.tensor_copy(
-                out=EB[u][:].rearrange("p (c i t) -> p c t i", i=4, t=4),
-                in_=E[u][:].rearrange("p t j (c i) -> p (j c) t i", i=4),
-            )
-
-        def fmul(u):
-            q, g, h = unit(u)
-            for jj in range(4):
-                j = 4 * h + jj
-                if j in BSET:
-                    e = E[u][:, :, jj, :]
-                    nc.vector.scalar_tensor_tensor(
-                        out=e, in0=x_sb[g][:, :, q * P : (q + 1) * P], scalar=grid_f[:, j : j + 1], in1=e,
-                        op0=ALU.subtract, op1=ALU.mult,
-                    )
-
-        def quant(u):
-            EC[u] = work.tile([P, 512], U32, name="ec", bufs=7, align_bytes=64)
-            ES[u] = work.tile([P, 512], U8, name="es", bufs=7, align_bytes=64)
-            nc.vector.quantize_mx(out=EC[u][:].bitcast(E4M3), scales=ES[u][:], in_=EB[u][:])
-
-        def dmm(u, t):
-            q, g, h = unit(u)
-            DT[u, t] = ps.tile([P, 512], F32, name="d", bufs=3)
-            c = slice(t * P, (t + 1) * P)
-            nc.tensor.matmul_mx(
-                out=DT[u, t][:], lhsT=got_c[g][:, c].bitcast(E5M2), lhsT_scale=got_s[g][:, c],
-                rhs=w_c[q][h][:].bitcast(E4M3), rhs_scale=w_s[q][h][:], start=True, stop=True,
-            )
-
-        def pmul(u, t):
-            if t == 0:
-                PP[u] = work.tile([P, 4, 4, P], F32, name="pp", bufs=3)
-            nc.vector.tensor_tensor(
-                out=PP[u][:, t].rearrange("p j i -> p (j i)"), in0=DT[u, t][:],
-                in1=E[u][:, t].rearrange("p j i -> p (j i)"), op=ALU.mult,
-            )
-
-        def gscale(u, eng):
-            h = u % 2
-            GP[u] = work.tile([P, 4, 4, P], F32, name="gp", bufs=2)
-            for jj in range(4):
-                j = 4 * h + jj
-                if j != REF and j not in BSET:
-                    (nc.vector if j in VSET else eng).tensor_scalar(
-                        out=GP[u][:, :, jj, :], in0=PP[u][:, :, jj, :], scalar1=grid_d[:, j : j + 1], scalar2=0.0,
-                        op0=ALU.mult, op1=ALU.add,
-                    )
-
-        def addt(out, src, first, last):
-            nc.tensor.matmul(out, lhsT=src, rhs=ident[:], start=first, stop=last, is_transpose=True)
-
-        def tsum0(u):
-            s, h = u // 2, u % 2
-            if h == 0:
-                TB[s] = ps.tile([P, 512], F32, name="t0", bufs=1)
-            js = [j for j in range(4 * h, 4 * h + 4) if j not in BSET]
-            for t in range(4):
-                for j in js:
-                    addt(
-                        TB[s][:, t * P : (t + 1) * P], PP[u][:, t, j % 4, :], h == 0 and t == 0 and j == js[0],
-                        h == 1 and t == 3 and j == js[-1],
-                    )
-
-        def tsum1(u):
-            s, h = u // 2, u % 2
-            if h == 0:
-                T1[s] = ps.tile([P, 512], F32, name="t1", bufs=1)
-            js = [j for j in range(4 * h, 4 * h + 4) if j != REF]
-            for t in range(4):
-                for j in js:
-                    src = PP[u] if j in BSET else GP[u]
-                    addt(
-                        T1[s][:, t * P : (t + 1) * P], src[:, t, j % 4, :], h == 0 and t == 0 and j == js[0],
-                        h == 1 and t == 3 and j == js[-1],
-                    )
-
-        def xtrans(q):
-            bank = ps.tile([P, 2, 4, P], BF16, name="m", bufs=3)
-            for g in range(2):
-                for t in range(4):
-                    nc.tensor.transpose(bank[:, g, t, :], x_sb[g][:, t, q * P : (q + 1) * P], ident_b[:])
-            return bank
-
-        def xevac(q, bank):
-            nc.scalar.copy(out=xt_sb[q][:].rearrange("p g c -> p (g c)"), in_=bank[:].rearrange("p g t c -> p (g t c)"))
-
-        def y0evac(s):
-            Y0[s] = work.tile([P, 512], F32, name="y0", bufs=2)
-            nc.vector.scalar_tensor_tensor(
-                out=Y0[s][:], in0=xt_sb[s // 2][:, s % 2, :], scalar=grid_f[:, REF : REF + 1], in1=TB[s][:],
-                op0=ALU.subtract, op1=ALU.mult,
-            )
-
-        def y1evac(s):
-            Y1[s] = work.tile([P, 512], F32, name="y1", bufs=2)
-            nc.scalar.copy(out=Y1[s][:], in_=T1[s][:])
-
-        def back(s):
-            BK[s] = ps.tile([P, 512], F32, name="m", bufs=3)
-            for k, y in ((0, Y0[s]), (1, Y1[s])):
-                for t in range(4):
-                    c = slice(t * P, (t + 1) * P)
-                    addt(BK[s][:, c], y[:, c], k == 0 and t == 0, k == 1 and t == 3)
-
-        def backevac(s):
-            q, g = s // 2, s % 2
-            o = work.tile([P, 4, P], F32, name="o0", bufs=3)
-            nc.scalar.activation(out=o[:].rearrange("p t i -> p (t i)"), in_=BK[s][:], func=ACT.Copy, scale=OUT_SCALE)
-            nc.sync.dma_start(out=o0_v[g][:, :, q * P : (q + 1) * P], in_=o[:])
-
-        def omm(q, j):
-            OP[q, j] = ps.tile([P, 512], F32, name="m", bufs=3)
-            h, jj = j // 4, j % 4
-            c = slice(jj * P, (jj + 1) * P)
-            for g in range(2):
-                u = 4 * q + 2 * g + h
-                nc.tensor.matmul_mx(
-                    out=OP[q, j][:], lhsT=EC[u][:, c].bitcast(E4M3), lhsT_scale=ES[u][:, c],
-                    rhs=gob_c[g][:].bitcast(E5M2), rhs_scale=gob_s[g][:], start=(g == 0), stop=(g == 1),
-                )
-
-        def oevac(q, j, eng="s"):
-            if j % 2 == 0:
-                OS[q, j // 2] = work.tile([P, 2, 512], F32, name="os", bufs=3)
-            st = OS[q, j // 2]
-            if eng == "s":
-                nc.scalar.copy(out=st[:, j % 2, :], in_=OP[q, j][:])
-            else:
-                nc.vector.tensor_copy(out=st[:, j % 2, :], in_=OP[q, j][:])
-            if j % 2 == 1:
-                nc.sync.dma_start(out=o1_v[q][:, j - 1 : j + 1, :], in_=st[:])
-
-        def words(src2d, bank, half):
-            w = src2d.bitcast(F32)
-            for r in range(2):
-                nc.tensor.transpose(bank[:, half, r, :], w[:, r : 256 : 2], ident[:])
-
-        def wtrans(q, h, k):
-            bank = ps.tile([P, 2, 2, P], F32, name="m", bufs=3)
+        def transpose_pairs(rows, k):
+            bank = psum.tile([P, 2, 2, P], F32, name="mixed", bufs=3)
             for a in range(2):
-                words(w_sb[q][h][:, 2 * k + a, :], bank, a)
+                pairs = rows[:, 2 * k + a, :].bitcast(F32)
+                for e in range(2):
+                    nc.tensor.transpose(bank[:, a, e, :], pairs[:, e : FEATURES // 2 : 2], identity[:])
             return bank
 
-        def spread(eng, dst, k, bank):
-            o = dst.bitcast(F32)[:, k * 512 : (k + 1) * 512].rearrange("p (a r e) -> p a r e", a=2, e=2)
+        def copy_pairs(engine, dst, k, bank):
+            o = dst.bitcast(F32)[:, k * BANK : (k + 1) * BANK].rearrange("p (a r e) -> p a r e", a=2, e=2)
             i = bank[:].rearrange("p a e r -> p a r e")
-            if eng == "s":
+            if engine == "scalar":
                 nc.scalar.copy(out=o, in_=i)
             else:
                 nc.vector.tensor_copy(out=o, in_=i)
 
-        def wtile(q, h):
-            WI[q, h] = work.tile([P, 2048], BF16, name="wi", bufs=3, align_bytes=64)
+        def new_paired(key):
+            paired[key] = work.tile([P, 4 * BANK], BF16, name="paired", bufs=3, align_bytes=64)
 
-        def wquant(q, h):
-            nc.vector.quantize_mx(out=w_c[q][h][:].bitcast(E4M3), scales=w_s[q][h][:], in_=WI[q, h][:])
+        def quantise_weight(c):
+            nc.vector.quantize_mx(out=w_codes[c][:].bitcast(E4M3), scales=w_scales[c][:], in_=paired["w", c][:])
 
-        def gtrans(g, k):
-            bank = ps.tile([P, 2, 2, P], F32, name="m", bufs=3)
-            for a in range(2):
-                words(go_sb[g][:, 2 * k + a, :], bank, a)
-            return bank
+        def quantise_grad_features(g):
+            nc.vector.quantize_mx(out=feat_codes[g][:].bitcast(E5M2), scales=feat_scales[g][:], in_=paired["g", g][:])
 
-        def gtquant(g):
-            nc.vector.quantize_mx(out=got_c[g][:].bitcast(E5M2), scales=got_s[g][:], in_=got_i[g][:])
 
-        def gbquant(g):
+        def interleave_grad(g):
+            for first in (0, FEATURES // 2):
+                cols = slice(first, first + FEATURES // 2)
+                nc.gpsimd.tensor_scalar(
+                    out=tok_in[g][:, cols, :].rearrange("p (c i) t -> p c t i", i=4),
+                    in0=grad_sb[g][:, :, cols].rearrange("p t (c i) -> p c t i", i=4),
+                    scalar1=1.0,
+                    scalar2=0.0,
+                    op0=ALU.mult,
+                    op1=ALU.add,
+                )
+
+        def quantise_grad_tokens(g):
             nc.vector.quantize_mx(
-                out=gob_c[g][:].bitcast(E5M2), scales=gob_s[g][:], in_=gob_i[g][:].rearrange("p o t -> p (o t)")
+                out=tok_codes[g][:].bitcast(E5M2),
+                scales=tok_scales[g][:],
+                in_=tok_in[g][:].rearrange("p o t -> p (o t)"),
             )
 
-        def ginter(g, part):
-            c = slice(part * 256, (part + 1) * 256)
-            nc.gpsimd.tensor_scalar(
-                out=gob_i[g][:, c, :].rearrange("p (c i) t -> p c t i", i=4),
-                in0=go_sb[g][:, :, c].rearrange("p t (c i) -> p c t i", i=4),
-                scalar1=1.0, scalar2=0.0, op0=ALU.mult, op1=ALU.add,
+
+        def square(u, jj):
+            q, g, h = unit(u)
+            if jj == 0:
+                basis[u] = work.tile([P, T, J, P], F32, name="basis", bufs=4)
+            j = J * h + jj
+            nc.scalar.activation(
+                out=basis[u][:, :, jj, :],
+                in_=x_sb[g][:, :, q * P : (q + 1) * P],
+                func=ACT.Square,
+                scale=INV_H,
+                bias=grid_bias[:, j : j + 1],
             )
+
+        def exponential(u):
+            flat = basis[u][:].rearrange("p t j i -> p (t j i)")
+            nc.scalar.activation(out=flat, in_=flat, func=ACT.Exp, scale=-1.0)
+
+        def round_basis(u):
+            rounded[u] = work.tile([P, 4 * BANK], BF16, name="rounded", bufs=2, align_bytes=64)
+            nc.vector.tensor_copy(
+                out=rounded[u][:].rearrange("p (c i t) -> p c t i", i=4, t=T),
+                in_=basis[u][:].rearrange("p t j (c i) -> p (j c) t i", i=4),
+            )
+
+        def quantise_basis(u):
+            codes[u] = work.tile([P, BANK], U32, name="codes", bufs=7, align_bytes=64)
+            scales[u] = work.tile([P, BANK], U8, name="scales", bufs=7, align_bytes=64)
+            nc.vector.quantize_mx(out=codes[u][:].bitcast(E4M3), scales=scales[u][:], in_=rounded[u][:])
+
+
+        def matmul_dbasis(u, t):
+            q, g, h = unit(u)
+            dbasis[u, t] = psum.tile([P, BANK], F32, name="dbasis", bufs=3)
+            cols = slice(t * P, (t + 1) * P)
+            nc.tensor.matmul_mx(
+                out=dbasis[u, t][:],
+                lhsT=feat_codes[g][:, cols].bitcast(E5M2),
+                lhsT_scale=feat_scales[g][:, cols],
+                rhs=w_codes[2 * q + h][:].bitcast(E4M3),
+                rhs_scale=w_scales[2 * q + h][:],
+                start=True,
+                stop=True,
+            )
+
+        def multiply(u, t):
+            if t == 0:
+                prod[u] = work.tile([P, T, J, P], F32, name="prod", bufs=3)
+            nc.vector.tensor_tensor(
+                out=prod[u][:, t].rearrange("p j i -> p (j i)"),
+                in0=dbasis[u, t][:],
+                in1=basis[u][:, t].rearrange("p j i -> p (j i)"),
+                op=ALU.mult,
+            )
+
+        def weigh(u):
+            engine = nc.gpsimd if u < UNITS - 1 else nc.vector
+            scaled[u] = work.tile([P, T, J, P], F32, name="scaled", bufs=2)
+            for jj in range(J):
+                j = J * (u % 2) + jj
+                if j != REF:
+                    engine.tensor_scalar(
+                        out=scaled[u][:, :, jj, :],
+                        in0=prod[u][:, :, jj, :],
+                        scalar1=grid_weight[:, j : j + 1],
+                        scalar2=0.0,
+                        op0=ALU.mult,
+                        op1=ALU.add,
+                    )
+
+        def add_transposed(out, src, first, last):
+            nc.tensor.matmul(out, lhsT=src, rhs=identity[:], start=first, stop=last, is_transpose=True)
+
+        def sum_grid_points(u, tokens, src, sums, name, points):
+            pair, h = u // 2, u % 2
+            here = [j for j in points if j // J == h]
+            if h == 0 and tokens[0] == 0:
+                sums[pair] = psum.tile([P, BANK], F32, name=name, bufs=1)
+            for t in tokens:
+                for j in here:
+                    add_transposed(
+                        sums[pair][:, t * P : (t + 1) * P],
+                        src[u][:, t, j % J, :],
+                        h == 0 and t == 0 and j == here[0],
+                        h == 1 and t == T - 1 and j == here[-1],
+                    )
+
+        def transpose_x(q):
+            bank = psum.tile([P, 2, T, P], BF16, name="mixed", bufs=3)
+            for g in range(2):
+                for t in range(T):
+                    nc.tensor.transpose(bank[:, g, t, :], x_sb[g][:, t, q * P : (q + 1) * P], identity_bf[:])
+            banks["x", q] = bank
+
+        def copy_x(q):
+            nc.scalar.copy(
+                out=x_t[q][:].rearrange("p g c -> p (g c)"), in_=banks["x", q][:].rearrange("p g t c -> p (g t c)")
+            )
+
+        def take_plain_sum(pair):
+            plain_sb[pair] = work.tile([P, BANK], F32, name="plain_sb", bufs=2)
+            nc.vector.scalar_tensor_tensor(
+                out=plain_sb[pair][:],
+                in0=x_t[pair // 2][:, pair % 2, :],
+                scalar=grid_f[:, REF : REF + 1],
+                in1=plain_sum[pair][:],
+                op0=ALU.subtract,
+                op1=ALU.mult,
+            )
+
+        def take_weighted_sum(pair):
+            weighted_sb[pair] = work.tile([P, BANK], F32, name="weighted_sb", bufs=2)
+            nc.scalar.copy(out=weighted_sb[pair][:], in_=weighted_sum[pair][:])
+
+        def transpose_back(pair):
+            result[pair] = psum.tile([P, BANK], F32, name="mixed", bufs=3)
+            for k, term in enumerate((plain_sb[pair], weighted_sb[pair])):
+                for t in range(T):
+                    cols = slice(t * P, (t + 1) * P)
+                    add_transposed(result[pair][:, cols], term[:, cols], k == 0 and t == 0, k == 1 and t == T - 1)
+
+        def store_out_0(pair):
+            q, g = pair // 2, pair % 2
+            o = work.tile([P, T, P], F32, name="out_0_sb", bufs=3)
+            nc.scalar.activation(
+                out=o[:].rearrange("p t i -> p (t i)"), in_=result[pair][:], func=ACT.Copy, scale=OUT_SCALE
+            )
+            nc.sync.dma_start(out=out_0_hbm[g][:, :, q * P : (q + 1) * P], in_=o[:])
+
+
+        def matmul_out_1(q, j):
+            acc[q, j] = psum.tile([P, BANK], F32, name="mixed", bufs=3)
+            h, jj = j // J, j % J
+            cols = slice(jj * P, (jj + 1) * P)
+            for g in range(2):
+                u = 4 * q + 2 * g + h
+                nc.tensor.matmul_mx(
+                    out=acc[q, j][:],
+                    lhsT=codes[u][:, cols].bitcast(E4M3),
+                    lhsT_scale=scales[u][:, cols],
+                    rhs=tok_codes[g][:].bitcast(E5M2),
+                    rhs_scale=tok_scales[g][:],
+                    start=(g == 0),
+                    stop=(g == 1),
+                )
+
+        def store_out_1(q, j, engine):
+            if j % 2 == 0:
+                staged[q, j // 2] = work.tile([P, 2, FEATURES], F32, name="staged", bufs=3)
+            s = staged[q, j // 2]
+            if engine == "scalar":
+                nc.scalar.copy(out=s[:, j % 2, :], in_=acc[q, j][:])
+            else:
+                nc.vector.tensor_copy(out=s[:, j % 2, :], in_=acc[q, j][:])
+            if j % 2 == 1:
+                nc.sync.dma_start(out=out_1_hbm[q][:, j - 1 : j + 1, :], in_=s[:])
+
+
+        def multiply_step(t):
+            return lambda n: multiply(n, t) if n < UNITS else None
+
+        def dbasis_step(t):
+            u_of = (lambda n: n + 1) if t < 3 else (lambda n: n)
+            return lambda n: matmul_dbasis(u_of(n), t) if u_of(n) < UNITS else None
+
+        def weigh_step(n):
+            if n < UNITS:
+                weigh(n)
+
+        def square_step(jj):
+            return lambda n: square(n + 2, jj) if n + 2 < UNITS else None
+
+        def exponential_step(n):
+            if n + 2 < UNITS:
+                exponential(n + 2)
+
+        def round_step(n):
+            if n + 1 < UNITS:
+                round_basis(n + 1)
+
+        def quantise_step(n):
+            if n + 1 < UNITS:
+                quantise_basis(n + 1)
+
+        def plain_step(tokens):
+            def step(n):
+                if 1 <= n <= UNITS:
+                    sum_grid_points(n - 1, tokens, prod, plain_sum, "plain", range(GRID))
+
+            return step
+
+        def weighted_step(n):
+            if 2 <= n <= UNITS + 1:
+                points = [j for j in range(GRID) if j != REF]
+                sum_grid_points(n - 2, range(T), scaled, weighted_sum, "weighted", points)
+
+        def pair_step(act, lag):
+            return lambda n: act((n - lag) // 2) if (n - lag) % 2 == 0 and 0 <= n - lag < UNITS else None
+
+        def out_1_products(n):
+            q, j = (n - 2) // 4, 2 * ((n - 2) % 4)
+            return [(q, j), (q, j + 1)] if 0 <= q < BLOCKS else []
+
+        def out_1_matmul_step(k):
+            def step(n):
+                for q, j in out_1_products(n)[k : k + 1]:
+                    matmul_out_1(q, j)
+
+            return step
+
+        def out_1_store_step(k):
+            def step(n):
+                engine = "vector" if k == 1 and n < UNITS - 2 else "scalar"
+                for q, j in out_1_products(n)[k : k + 1]:
+                    store_out_1(q, j, engine)
+
+            return step
+
+
+        def weight_transpose_step(n):
+            c, k = n // 2 + 2, n % 2
+            if c < 2 * BLOCKS:
+                if k == 0:
+                    new_paired(("w", c))
+                banks["w", n] = transpose_pairs(w_raw[c], k)
+
+        def weight_copy_step(n):
+            c, k = n // 2 + 2, n % 2
+            if c < 2 * BLOCKS:
+                copy_pairs("scalar" if k == 0 else "vector", paired["w", c][:], k, banks["w", n])
+
+        def weight_quantise_step(n):
+            c, k = n // 2 + 2, n % 2
+            if c < 2 * BLOCKS and k == 1:
+                quantise_weight(c)
+
+        def x_transpose_step(n):
+            if n < BLOCKS:
+                transpose_x(n)
+
+        def x_copy_step(n):
+            if n < BLOCKS:
+                copy_x(n)
+
+
+        def second_chunk_copy(n):
+            copy_pairs("scalar", paired["w", 1][:], 1, banks["second chunk"])
+
+        def second_chunk_quantise(n):
+            quantise_weight(1)
+
+        def first_round(n):
+            round_basis(0)
+
+        def first_quantise(n):
+            quantise_basis(0)
+
+        def second_half_transpose(n):
+            new_paired(("g", 1))
+            for k in range(2):
+                copy_pairs("scalar", paired["g", 1][:], k, transpose_pairs(grad_sb[1], k))
+
+        def second_half_quantise(n):
+            quantise_grad_features(1)
+
+        def second_half_interleave(n):
+            interleave_grad(1)
+
+        def grad_tokens_quantise(n):
+            quantise_grad_tokens(0)
+            quantise_grad_tokens(1)
+
+        mul_0, mul_1, mul_2, mul_3 = [multiply_step(t) for t in range(T)]
+        dba_0, dba_1, dba_2, dba_3 = [dbasis_step(t) for t in range(T)]
+        squ_0, squ_1, squ_2, squ_3 = [square_step(jj) for jj in range(J)]
+        plain_low, plain_high = plain_step((0, 1)), plain_step((2, 3))
+        o1_mm_0, o1_mm_1 = out_1_matmul_step(0), out_1_matmul_step(1)
+        o1_st_0, o1_st_1 = out_1_store_step(0), out_1_store_step(1)
+        take_plain, take_weighted = pair_step(take_plain_sum, 2), pair_step(take_weighted_sum, 3)
+        back, store_0 = pair_step(transpose_back, 5), pair_step(store_out_0, 5)
+
+        steady = (
+            o1_mm_0, o1_st_0, o1_mm_1, x_transpose_step, mul_0, dba_3, weighted_step, mul_1, mul_2, o1_st_1,
+            weight_transpose_step, squ_0, plain_low, squ_1, round_step, mul_3, squ_2, plain_high, back, squ_3,
+            weight_copy_step, take_weighted, x_copy_step, weigh_step, weight_quantise_step, quantise_step,
+            dba_0, dba_1, exponential_step, dba_2, store_0, take_plain,
+        )
+        slot_0 = (
+            weight_transpose_step, mul_0, second_half_interleave, first_round, round_step, second_chunk_copy,
+            second_half_transpose, mul_1, x_transpose_step, second_half_quantise, dba_3, mul_2, weight_copy_step,
+            quantise_step, second_chunk_quantise, dba_0, mul_3, dba_1, squ_0, weigh_step, squ_1, first_quantise, dba_2,
+            squ_2, squ_3, x_copy_step, exponential_step,
+        )
+        slot_1 = (
+            weight_transpose_step, mul_0, x_transpose_step, mul_1, squ_0, mul_2, squ_1, plain_low, x_copy_step, dba_3,
+            dba_0, squ_2, dba_1, dba_2, weight_copy_step, round_step, mul_3, squ_3, plain_high, grad_tokens_quantise,
+            weigh_step, quantise_step, weight_quantise_step, exponential_step,
+        )
 
         with tc.manual_schedule():
-            nc.gpsimd.memset(warm[:], 0.0)
+            nc.gpsimd.memset(one_column[:], 0.0)
             nc.scalar.dma_start(out=grid_bf[:], in_=grid.partition_broadcast(P))
-            nc.scalar.activation(out=warm[:], in_=warm[:], func=ACT.Exp)
-            nc.sync.dma_start(out=x_sb[0][:], in_=x_v[0])
-            nc.sync.dma_start(out=go_sb[0][:], in_=go_v[0])
-            nc.sync.dma_start(out=w_sb[0][0][:], in_=w_v[0][:, 0:4, :])
-            nc.sync.dma_start(out=w_sb[0][1][:], in_=w_v[0][:, 4:8, :])
-            nc.sync.dma_start(out=go_sb[1][:], in_=go_v[1])
-            nc.sync.dma_start(out=x_sb[1][:], in_=x_v[1])
-            for q in range(1, 4):
-                for h in range(2):
-                    nc.sync.dma_start(out=w_sb[q][h][:], in_=w_v[q][:, 4 * h : 4 * h + 4, :])
-            make_identity(nc, ident[:])
-            make_identity(nc, ident_b[:])
-            nc.vector.tensor_scalar(out=grid_n[:], in0=grid_bf[:], scalar1=-INV_H, scalar2=None, op0=ALU.mult)
+            nc.scalar.activation(out=one_column[:], in_=one_column[:], func=ACT.Exp)
+
+            nc.sync.dma_start(out=x_sb[0][:], in_=x_hbm[0])
+            nc.sync.dma_start(out=grad_sb[0][:], in_=grad_hbm[0])
+            load_weight(0)
+            load_weight(1)
+            nc.sync.dma_start(out=grad_sb[1][:], in_=grad_hbm[1])
+            nc.sync.dma_start(out=x_sb[1][:], in_=x_hbm[1])
+            for c in range(2, 2 * BLOCKS):
+                load_weight(c)
+
+            make_identity(nc, identity[:])
+            make_identity(nc, identity_bf[:])
+            nc.vector.tensor_scalar(
+                out=grid_bias[:], in0=grid_bf[:], scalar1=-INV_H, scalar2=None, op0=ALU.mult
+            )
             nc.vector.tensor_copy(out=grid_f[:], in_=grid_bf[:])
             nc.vector.tensor_scalar(
-                out=grid_d[:], in0=grid_f[:], scalar1=grid_f[:, REF : REF + 1], scalar2=-1.0, op0=ALU.subtract, op1=ALU.mult
+                out=grid_weight[:],
+                in0=grid_f[:],
+                scalar1=grid_f[:, REF : REF + 1],
+                scalar2=-1.0,
+                op0=ALU.subtract,
+                op1=ALU.mult,
             )
 
-            for jj in range(4):
-                sq(0, jj)
-            exp(0)
-            got_i[0] = work.tile([P, 2048], BF16, name="wi", bufs=3, align_bytes=64)
+            for key in (("g", 0), ("w", 0), ("w", 1)):
+                new_paired(key)
+            for jj in range(J):
+                square(0, jj)
+            exponential(0)
             for k in range(2):
-                spread("v", got_i[0][:], k, gtrans(0, k))
-            wtile(0, 0)
-            spread("v", WI[0, 0][:], 0, wtrans(0, 0, 0))
-            gtquant(0)
-            spread("v", WI[0, 0][:], 1, wtrans(0, 0, 1))
-            wtile(0, 1)
-            wbank = [wtrans(0, 1, 0), wtrans(0, 1, 1)]
-            ginter(0, 0)
-            ginter(0, 1)
-            wquant(0, 0)
+                copy_pairs("vector", paired["g", 0][:], k, transpose_pairs(grad_sb[0], k))
+            quantise_grad_features(0)
+            for k in range(2):
+                copy_pairs("vector", paired["w", 0][:], k, transpose_pairs(w_raw[0], k))
+            second_chunk = [transpose_pairs(w_raw[1], k) for k in range(2)]
+            quantise_weight(0)
             for t in range(3):
-                dmm(0, t)
-            for jj in range(4):
-                sq(1, jj)
-            spread("s", WI[0, 1][:], 0, wbank[0])
-            exp(1)
+                matmul_dbasis(0, t)
+            interleave_grad(0)
+            for jj in range(J):
+                square(1, jj)
+            exponential(1)
+            copy_pairs("vector", paired["w", 1][:], 0, second_chunk[0])
+            banks["second chunk"] = second_chunk[1]
 
-            o_slots = {}
-            for q in range(4):
-                for j in range(8):
-                    n = 4 * q + 2 + j // 2 if q < 3 else (14 if j < 4 else 15)
-                    o_slots.setdefault(n, []).append((q, j))
-
-            for n in range(UNITS + 3):
-                live = n < UNITS
-                nxt = n + 1 < UNITS
-                todo = o_slots.get(n, [])
-                wq, wh, wk = n // 4 + 1, (n // 2) % 2, n % 2
-                if live:
-                    pmul(n, 0)
-                for q, j in todo[:2]:
-                    omm(q, j)
-                if live:
-                    dmm(n, 3)
-                if n + 2 < UNITS:
-                    sq(n + 2, 0)
-                    sq(n + 2, 1)
-                if live:
-                    pmul(n, 1)
-                    pmul(n, 2)
-                    pmul(n, 3)
-                    gscale(n, nc.gpsimd if n < UNITS - 1 else nc.vector)
-                if n == 0:
-                    cast(0)
-                    spread("v", WI[0, 1][:], 1, wbank[1])
-                    quant(0)
-                    wquant(0, 1)
-                if 1 <= n <= UNITS:
-                    tsum0(n - 1)
-                if 2 <= n <= UNITS + 1:
-                    tsum1(n - 2)
-                if n % 2 == 0 and n >= 4:
-                    back((n - 4) // 2)
-                if n == 0:
-                    got_i[1] = work.tile([P, 2048], BF16, name="wi", bufs=3, align_bytes=64)
-                    spread("v", got_i[1][:], 0, gtrans(1, 0))
-                    spread("v", got_i[1][:], 1, gtrans(1, 1))
-                bank = None
-                if wq < 4:
-                    if wk == 0:
-                        wtile(wq, wh)
-                    bank = wtrans(wq, wh, wk)
-                if n % 4 == 1 and live:
-                    xbank = xtrans(n // 4)
-                if nxt:
-                    for t in range(3):
-                        dmm(n + 1, t)
-                for k, (q, j) in enumerate(todo[:2]):
-                    oevac(q, j, "sv"[k])
-                if n % 4 == 1 and live:
-                    xevac(n // 4, xbank)
-                if n == 0:
-                    ginter(1, 0)
-                    ginter(1, 1)
-                if nxt:
-                    cast(n + 1)
-                    fmul(n + 1)
-                if n + 2 < UNITS:
-                    sq(n + 2, 2)
-                    sq(n + 2, 3)
-                if bank is not None:
-                    spread("sv"[wk], WI[wq, wh][:], wk, bank)
-                if n % 2 == 0 and 2 <= n <= UNITS:
-                    y0evac((n - 2) // 2)
-                if n % 2 == 1 and 3 <= n:
-                    y1evac((n - 3) // 2)
-                if n % 2 == 0 and n >= 4:
-                    backevac((n - 4) // 2)
-                if n + 2 < UNITS:
-                    exp(n + 2)
-                if n == 0:
-                    gtquant(1)
-                if n == 1:
-                    gbquant(0)
-                    gbquant(1)
-                if nxt:
-                    quant(n + 1)
-                if wq < 4 and wk == 1:
-                    wquant(wq, wh)
-                for q, j in todo[2:]:
-                    omm(q, j)
-                    oevac(q, j)
+            for n in range(UNITS + 4):
+                for step in {0: slot_0, 1: slot_1}.get(n, steady):
+                    step(n)

@@ -139,10 +139,13 @@ def tile_gaussiankernel_v_kernel(tc, x, grid, spline_weight, grad_out, out_0, ou
 
         def round_basis(u):
             rounded[u] = work.tile([P, 4 * BANK], BF16, name="rounded", bufs=2, align_bytes=64)
-            nc.vector.tensor_copy(
-                out=rounded[u][:].rearrange("p (c i t) -> p c t i", i=4, t=T),
-                in_=basis[u][:].rearrange("p t j (c i) -> p (j c) t i", i=4),
+            dst = rounded[u][:].rearrange("p (c i t) -> p c t i", i=4, t=T)
+            src = basis[u][:].rearrange("p t j (c i) -> p (j c) t i", i=4)
+            first = P // 4
+            nc.gpsimd.tensor_scalar(
+                out=dst[:, :first], in0=src[:, :first], scalar1=1.0, scalar2=0.0, op0=ALU.mult, op1=ALU.add
             )
+            nc.vector.tensor_copy(out=dst[:, first:], in_=src[:, first:])
 
         def quantise_basis(u):
             codes[u] = work.tile([P, BANK], U32, name="codes", bufs=7, align_bytes=64)
@@ -243,8 +246,12 @@ def tile_gaussiankernel_v_kernel(tc, x, grid, spline_weight, grad_out, out_0, ou
         def store_out_0(pair):
             q, g = pair // 2, pair % 2
             o = work.tile([P, T, P], F32, name="out_0_sb", bufs=3)
-            nc.scalar.activation(
-                out=o[:].rearrange("p t i -> p (t i)"), in_=result[pair][:], func=ACT.Copy, scale=OUT_SCALE
+            nc.vector.tensor_scalar(
+                out=o[:].rearrange("p t i -> p (t i)"),
+                in0=result[pair][:],
+                scalar1=OUT_SCALE,
+                scalar2=None,
+                op0=ALU.mult,
             )
             nc.sync.dma_start(out=out_0_hbm[g][:, :, q * P : (q + 1) * P], in_=o[:])
 
@@ -331,7 +338,7 @@ def tile_gaussiankernel_v_kernel(tc, x, grid, spline_weight, grad_out, out_0, ou
 
         def out_1_store_step(k):
             def step(n):
-                engine = "vector" if k == 1 and n < UNITS - 2 else "scalar"
+                engine = "scalar" if k == 0 else "vector"
                 for q, j in out_1_products(n)[k : k + 1]:
                     store_out_1(q, j, engine)
 
@@ -365,7 +372,7 @@ def tile_gaussiankernel_v_kernel(tc, x, grid, spline_weight, grad_out, out_0, ou
 
 
         def second_chunk_copy(n):
-            copy_pairs("scalar", paired["w", 1][:], 1, banks["second chunk"])
+            copy_pairs("vector", paired["w", 1][:], 1, banks["second chunk"])
 
         def second_chunk_quantise(n):
             quantise_weight(1)
@@ -379,7 +386,7 @@ def tile_gaussiankernel_v_kernel(tc, x, grid, spline_weight, grad_out, out_0, ou
         def second_half_transpose(n):
             new_paired(("g", 1))
             for k in range(2):
-                copy_pairs("scalar", paired["g", 1][:], k, transpose_pairs(grad_sb[1], k))
+                copy_pairs("vector" if k == 0 else "scalar", paired["g", 1][:], k, transpose_pairs(grad_sb[1], k))
 
         def second_half_quantise(n):
             quantise_grad_features(1)
@@ -401,21 +408,21 @@ def tile_gaussiankernel_v_kernel(tc, x, grid, spline_weight, grad_out, out_0, ou
         back, store_0 = pair_step(transpose_back, 5), pair_step(store_out_0, 5)
 
         steady = (
-            o1_mm_0, o1_st_0, o1_mm_1, x_transpose_step, mul_0, dba_3, weighted_step, mul_1, mul_2, o1_st_1,
-            weight_transpose_step, squ_0, plain_low, squ_1, round_step, mul_3, squ_2, plain_high, back, squ_3,
-            weight_copy_step, take_weighted, x_copy_step, weigh_step, weight_quantise_step, quantise_step,
-            dba_0, dba_1, exponential_step, dba_2, store_0, take_plain,
+            squ_0, mul_0, x_transpose_step, o1_mm_0, x_copy_step, o1_mm_1, dba_3, squ_1, weighted_step,
+            weight_transpose_step, mul_1, mul_2, plain_low, squ_2, o1_st_0, back, plain_high, squ_3, o1_st_1, round_step,
+            mul_3, quantise_step, take_weighted, weigh_step, weight_copy_step, store_0, dba_0, exponential_step, dba_1,
+            dba_2, take_plain, weight_quantise_step,
         )
         slot_0 = (
-            weight_transpose_step, mul_0, second_half_interleave, first_round, round_step, second_chunk_copy,
-            second_half_transpose, mul_1, x_transpose_step, second_half_quantise, dba_3, mul_2, weight_copy_step,
-            quantise_step, second_chunk_quantise, dba_0, mul_3, dba_1, squ_0, weigh_step, squ_1, first_quantise, dba_2,
-            squ_2, squ_3, x_copy_step, exponential_step,
+            second_chunk_copy, dba_3, mul_0, second_half_interleave, mul_1, first_round, squ_0, second_chunk_quantise, squ_1,
+            weight_transpose_step, second_half_transpose, squ_2, x_transpose_step, round_step, squ_3, dba_0, mul_2, dba_1,
+            first_quantise, dba_2, weight_copy_step, mul_3, exponential_step, weigh_step, quantise_step, x_copy_step,
+            second_half_quantise,
         )
         slot_1 = (
-            weight_transpose_step, mul_0, x_transpose_step, mul_1, squ_0, mul_2, squ_1, plain_low, x_copy_step, dba_3,
-            dba_0, squ_2, dba_1, dba_2, weight_copy_step, round_step, mul_3, squ_3, plain_high, grad_tokens_quantise,
-            weigh_step, quantise_step, weight_quantise_step, exponential_step,
+            weight_transpose_step, grad_tokens_quantise, squ_0, plain_low, x_transpose_step, plain_high, round_step, dba_3,
+            mul_0, dba_0, mul_1, dba_1, weight_copy_step, squ_1, mul_2, mul_3, quantise_step, squ_2, weigh_step,
+            weight_quantise_step, dba_2, squ_3, x_copy_step, exponential_step,
         )
 
         with tc.manual_schedule():

from contextlib import ExitStack

import concourse.mybir as mybir
from concourse.masks import make_identity

F32 = mybir.dt.float32
BF16 = mybir.dt.bfloat16
U32 = mybir.dt.uint32
U8 = mybir.dt.uint8
E4M3 = mybir.dt.float8_e4m3fn_x4
E5M2 = mybir.dt.float8_e5m2_x4
ACT = mybir.ActivationFunctionType
ALU = mybir.AluOpType

TOKENS, INPUTS, GRID, FEATURES = 1024, 512, 8, 512
FLOPS = 2 * 2 * TOKENS * INPUTS * GRID * FEATURES

P = 128
T = 4
J = 4
BANK = 512
UNITS = 16
BLOCKS = 4
INV_H = 7.0 / 4.0
OUT_SCALE = -2.0 * INV_H * INV_H
REF = 3


def tile_gaussiankernel_v_kernel(tc, x, grid, spline_weight, grad_out, out_0, out_1):
    nc = tc.nc

    x_hbm = x.rearrange("(g p t) i -> g p t i", g=2, t=T)
    grad_hbm = grad_out.rearrange("(g p t) o -> g p t o", g=2, t=T)
    weight_hbm = spline_weight.rearrange("(q p j) o -> q p j o", q=BLOCKS, j=GRID)
    out_0_hbm = out_0.rearrange("(g p t) i -> g p t i", g=2, t=T)
    out_1_hbm = out_1.rearrange("(q p j) o -> q p j o", q=BLOCKS, j=GRID)

    with ExitStack() as ctx:
        keep = ctx.enter_context(tc.tile_pool(name="keep", bufs=1))
        work = ctx.enter_context(tc.tile_pool(name="work", bufs=2))
        psum = ctx.enter_context(tc.psum_pool(name="psum", bufs=1))

        identity = keep.tile([P, P], F32, name="identity")
        identity_bf = keep.tile([P, P], BF16, name="identity_bf")
        grid_bf = keep.tile([P, GRID], BF16, name="grid_bf")
        grid_f = keep.tile([P, GRID], F32, name="grid_f")
        grid_bias = keep.tile([P, GRID], F32, name="grid_bias")
        grid_weight = keep.tile([P, GRID], F32, name="grid_weight")
        one_column = keep.tile([P, 1], F32, name="one_column")
        x_sb = [keep.tile([P, T, INPUTS], BF16, name="x%d" % g) for g in range(2)]
        x_t = [keep.tile([P, 2, BANK], BF16, name="xt%d" % q) for q in range(BLOCKS)]
        grad_sb = [keep.tile([P, T, FEATURES], BF16, name="grad%d" % g, align_bytes=64) for g in range(2)]

        tok_in = [keep.tile([P, FEATURES, T], BF16, name="toki%d" % g, align_bytes=64) for g in range(2)]
        tok_codes = [keep.tile([P, FEATURES], U32, name="tokc%d" % g, align_bytes=64) for g in range(2)]
        tok_scales = [keep.tile([P, FEATURES], U8, name="toks%d" % g, align_bytes=64) for g in range(2)]
        feat_codes = [keep.tile([P, BANK], U32, name="featc%d" % g, align_bytes=64) for g in range(2)]
        feat_scales = [keep.tile([P, BANK], U8, name="feats%d" % g, align_bytes=64) for g in range(2)]
        w_codes = [keep.tile([P, BANK], U32, name="wc%d" % c, align_bytes=64) for c in range(2 * BLOCKS)]
        w_scales = [keep.tile([P, BANK], U8, name="ws%d" % c, align_bytes=64) for c in range(2 * BLOCKS)]

        w_raw, paired, banks = {}, {}, {}
        basis, rounded, codes, scales = {}, {}, {}, {}
        dbasis, prod, scaled = {}, {}, {}
        plain_sum, weighted_sum, plain_sb, weighted_sb, result = {}, {}, {}, {}, {}
        acc, staged = {}, {}

        def unit(u):
            return u // 4, (u // 2) % 2, u % 2


        def load_weight(c):
            w_raw[c] = work.tile([P, J, FEATURES], BF16, name="w_raw", bufs=5, align_bytes=64)
            first = J * (c % 2)
            nc.sync.dma_start(out=w_raw[c][:], in_=weight_hbm[c // 2][:, first : first + J, :])

        def transpose_pairs(rows, k):
            bank = psum.tile([P, 2, 2, P], F32, name="mixed", bufs=3)
            for a in range(2):
                pairs = rows[:, 2 * k + a, :].bitcast(F32)
                for e in range(2):
                    nc.tensor.transpose(bank[:, a, e, :], pairs[:, e : FEATURES // 2 : 2], identity[:])
            return bank

        def copy_pairs(engine, dst, k, bank):
            o = dst.bitcast(F32)[:, k * BANK : (k + 1) * BANK].rearrange("p (a r e) -> p a r e", a=2, e=2)
            i = bank[:].rearrange("p a e r -> p a r e")
            if engine == "scalar":
                nc.scalar.copy(out=o, in_=i)
            else:
                nc.vector.tensor_copy(out=o, in_=i)

        def new_paired(key):
            paired[key] = work.tile([P, 4 * BANK], BF16, name="paired", bufs=3, align_bytes=64)

        def quantise_weight(c):
            nc.vector.quantize_mx(out=w_codes[c][:].bitcast(E4M3), scales=w_scales[c][:], in_=paired["w", c][:])

        def quantise_grad_features(g):
            nc.vector.quantize_mx(out=feat_codes[g][:].bitcast(E5M2), scales=feat_scales[g][:], in_=paired["g", g][:])


        def interleave_grad(g):
            for first in (0, FEATURES // 2):
                cols = slice(first, first + FEATURES // 2)
                nc.gpsimd.tensor_scalar(
                    out=tok_in[g][:, cols, :].rearrange("p (c i) t -> p c t i", i=4),
                    in0=grad_sb[g][:, :, cols].rearrange("p t (c i) -> p c t i", i=4),
                    scalar1=1.0,
                    scalar2=0.0,
                    op0=ALU.mult,
                    op1=ALU.add,
                )

        def quantise_grad_tokens(g):
            nc.vector.quantize_mx(
                out=tok_codes[g][:].bitcast(E5M2),
                scales=tok_scales[g][:],
                in_=tok_in[g][:].rearrange("p o t -> p (o t)"),
            )


        def square(u, jj):
            q, g, h = unit(u)
            if jj == 0:
                basis[u] = work.tile([P, T, J, P], F32, name="basis", bufs=4)
            j = J * h + jj
            nc.scalar.activation(
                out=basis[u][:, :, jj, :],
                in_=x_sb[g][:, :, q * P : (q + 1) * P],
                func=ACT.Square,
                scale=INV_H,
                bias=grid_bias[:, j : j + 1],
            )

        def exponential(u):
            flat = basis[u][:].rearrange("p t j i -> p (t j i)")
            nc.scalar.activation(out=flat, in_=flat, func=ACT.Exp, scale=-1.0)

        def round_basis(u):
            rounded[u] = work.tile([P, 4 * BANK], BF16, name="rounded", bufs=2, align_bytes=64)
            dst = rounded[u][:].rearrange("p (c i t) -> p c t i", i=4, t=T)
            src = basis[u][:].rearrange("p t j (c i) -> p (j c) t i", i=4)
            first = P // 4
            nc.gpsimd.tensor_scalar(
                out=dst[:, :first], in0=src[:, :first], scalar1=1.0, scalar2=0.0, op0=ALU.mult, op1=ALU.add
            )
            nc.vector.tensor_copy(out=dst[:, first:], in_=src[:, first:])

        def quantise_basis(u):
            codes[u] = work.tile([P, BANK], U32, name="codes", bufs=7, align_bytes=64)
            scales[u] = work.tile([P, BANK], U8, name="scales", bufs=7, align_bytes=64)
            nc.vector.quantize_mx(out=codes[u][:].bitcast(E4M3), scales=scales[u][:], in_=rounded[u][:])


        def matmul_dbasis(u, t):
            q, g, h = unit(u)
            dbasis[u, t] = psum.tile([P, BANK], F32, name="dbasis", bufs=3)
            cols = slice(t * P, (t + 1) * P)
            nc.tensor.matmul_mx(
                out=dbasis[u, t][:],
                lhsT=feat_codes[g][:, cols].bitcast(E5M2),
                lhsT_scale=feat_scales[g][:, cols],
                rhs=w_codes[2 * q + h][:].bitcast(E4M3),
                rhs_scale=w_scales[2 * q + h][:],
                start=True,
                stop=True,
            )

        def multiply(u, t):
            if t == 0:
                prod[u] = work.tile([P, T, J, P], F32, name="prod", bufs=3)
            nc.vector.tensor_tensor(
                out=prod[u][:, t].rearrange("p j i -> p (j i)"),
                in0=dbasis[u, t][:],
                in1=basis[u][:, t].rearrange("p j i -> p (j i)"),
                op=ALU.mult,
            )

        def weigh(u):
            engine = nc.gpsimd if u < UNITS - 1 else nc.vector
            scaled[u] = work.tile([P, T, J, P], F32, name="scaled", bufs=2)
            for jj in range(J):
                j = J * (u % 2) + jj
                if j != REF:
                    engine.tensor_scalar(
                        out=scaled[u][:, :, jj, :],
                        in0=prod[u][:, :, jj, :],
                        scalar1=grid_weight[:, j : j + 1],
                        scalar2=0.0,
                        op0=ALU.mult,
                        op1=ALU.add,
                    )

        def add_transposed(out, src, first, last):
            nc.tensor.matmul(out, lhsT=src, rhs=identity[:], start=first, stop=last, is_transpose=True)

        def sum_grid_points(u, tokens, src, sums, name, points):
            pair, h = u // 2, u % 2
            here = [j for j in points if j // J == h]
            if h == 0 and tokens[0] == 0:
                sums[pair] = psum.tile([P, BANK], F32, name=name, bufs=1)
            for t in tokens:
                for j in here:
                    add_transposed(
                        sums[pair][:, t * P : (t + 1) * P],
                        src[u][:, t, j % J, :],
                        h == 0 and t == 0 and j == here[0],
                        h == 1 and t == T - 1 and j == here[-1],
                    )

        def transpose_x(q):
            bank = psum.tile([P, 2, T, P], BF16, name="mixed", bufs=3)
            for g in range(2):
                for t in range(T):
                    nc.tensor.transpose(bank[:, g, t, :], x_sb[g][:, t, q * P : (q + 1) * P], identity_bf[:])
            banks["x", q] = bank

        def copy_x(q):
            nc.scalar.copy(
                out=x_t[q][:].rearrange("p g c -> p (g c)"), in_=banks["x", q][:].rearrange("p g t c -> p (g t c)")
            )

        def take_plain_sum(pair):
            plain_sb[pair] = work.tile([P, BANK], F32, name="plain_sb", bufs=2)
            nc.vector.scalar_tensor_tensor(
                out=plain_sb[pair][:],
                in0=x_t[pair // 2][:, pair % 2, :],
                scalar=grid_f[:, REF : REF + 1],
                in1=plain_sum[pair][:],
                op0=ALU.subtract,
                op1=ALU.mult,
            )

        def take_weighted_sum(pair):
            weighted_sb[pair] = work.tile([P, BANK], F32, name="weighted_sb", bufs=2)
            nc.scalar.copy(out=weighted_sb[pair][:], in_=weighted_sum[pair][:])

        def transpose_back(pair):
            result[pair] = psum.tile([P, BANK], F32, name="mixed", bufs=3)
            for k, term in enumerate((plain_sb[pair], weighted_sb[pair])):
                for t in range(T):
                    cols = slice(t * P, (t + 1) * P)
                    add_transposed(result[pair][:, cols], term[:, cols], k == 0 and t == 0, k == 1 and t == T - 1)

        def store_out_0(pair):
            q, g = pair // 2, pair % 2
            o = work.tile([P, T, P], F32, name="out_0_sb", bufs=3)
            nc.vector.tensor_scalar(
                out=o[:].rearrange("p t i -> p (t i)"),
                in0=result[pair][:],
                scalar1=OUT_SCALE,
                scalar2=None,
                op0=ALU.mult,
            )
            nc.sync.dma_start(out=out_0_hbm[g][:, :, q * P : (q + 1) * P], in_=o[:])


        def matmul_out_1(q, j):
            acc[q, j] = psum.tile([P, BANK], F32, name="mixed", bufs=3)
            h, jj = j // J, j % J
            cols = slice(jj * P, (jj + 1) * P)
            for g in range(2):
                u = 4 * q + 2 * g + h
                nc.tensor.matmul_mx(
                    out=acc[q, j][:],
                    lhsT=codes[u][:, cols].bitcast(E4M3),
                    lhsT_scale=scales[u][:, cols],
                    rhs=tok_codes[g][:].bitcast(E5M2),
                    rhs_scale=tok_scales[g][:],
                    start=(g == 0),
                    stop=(g == 1),
                )

        def store_out_1(q, j, engine):
            if j % 2 == 0:
                staged[q, j // 2] = work.tile([P, 2, FEATURES], F32, name="staged", bufs=3)
            s = staged[q, j // 2]
            if engine == "scalar":
                nc.scalar.copy(out=s[:, j % 2, :], in_=acc[q, j][:])
            else:
                nc.vector.tensor_copy(out=s[:, j % 2, :], in_=acc[q, j][:])
            if j % 2 == 1:
                nc.sync.dma_start(out=out_1_hbm[q][:, j - 1 : j + 1, :], in_=s[:])


        def multiply_step(t):
            return lambda n: multiply(n, t) if n < UNITS else None

        def dbasis_step(t):
            u_of = (lambda n: n + 1) if t < 3 else (lambda n: n)
            return lambda n: matmul_dbasis(u_of(n), t) if u_of(n) < UNITS else None

        def weigh_step(n):
            if n < UNITS:
                weigh(n)

        def square_step(jj):
            return lambda n: square(n + 2, jj) if n + 2 < UNITS else None

        def exponential_step(n):
            if n + 2 < UNITS:
                exponential(n + 2)

        def round_step(n):
            if n + 1 < UNITS:
                round_basis(n + 1)

        def quantise_step(n):
            if n + 1 < UNITS:
                quantise_basis(n + 1)

        def plain_step(tokens):
            def step(n):
                if 1 <= n <= UNITS:
                    sum_grid_points(n - 1, tokens, prod, plain_sum, "plain", range(GRID))

            return step

        def weighted_step(n):
            if 2 <= n <= UNITS + 1:
                points = [j for j in range(GRID) if j != REF]
                sum_grid_points(n - 2, range(T), scaled, weighted_sum, "weighted", points)

        def pair_step(act, lag):
            return lambda n: act((n - lag) // 2) if (n - lag) % 2 == 0 and 0 <= n - lag < UNITS else None

        def out_1_products(n):
            q, j = (n - 2) // 4, 2 * ((n - 2) % 4)
            return [(q, j), (q, j + 1)] if 0 <= q < BLOCKS else []

        def out_1_matmul_step(k):
            def step(n):
                for q, j in out_1_products(n)[k : k + 1]:
                    matmul_out_1(q, j)

            return step

        def out_1_store_step(k):
            def step(n):
                engine = "scalar" if k == 0 else "vector"
                for q, j in out_1_products(n)[k : k + 1]:
                    store_out_1(q, j, engine)

            return step


        def weight_transpose_step(n):
            c, k = n // 2 + 2, n % 2
            if c < 2 * BLOCKS:
                if k == 0:
                    new_paired(("w", c))
                banks["w", n] = transpose_pairs(w_raw[c], k)

        def weight_copy_step(n):
            c, k = n // 2 + 2, n % 2
            if c < 2 * BLOCKS:
                copy_pairs("scalar" if k == 0 else "vector", paired["w", c][:], k, banks["w", n])

        def weight_quantise_step(n):
            c, k = n // 2 + 2, n % 2
            if c < 2 * BLOCKS and k == 1:
                quantise_weight(c)

        def x_transpose_step(n):
            if n < BLOCKS:
                transpose_x(n)

        def x_copy_step(n):
            if n < BLOCKS:
                copy_x(n)


        def second_chunk_copy(n):
            copy_pairs("vector", paired["w", 1][:], 1, banks["second chunk"])

        def second_chunk_quantise(n):
            quantise_weight(1)

        def first_round(n):
            round_basis(0)

        def first_quantise(n):
            quantise_basis(0)

        def second_half_transpose(n):
            new_paired(("g", 1))
            for k in range(2):
                copy_pairs("vector" if k == 0 else "scalar", paired["g", 1][:], k, transpose_pairs(grad_sb[1], k))

        def second_half_quantise(n):
            quantise_grad_features(1)

        def second_half_interleave(n):
            interleave_grad(1)

        def grad_tokens_quantise(n):
            quantise_grad_tokens(0)
            quantise_grad_tokens(1)

        mul_0, mul_1, mul_2, mul_3 = [multiply_step(t) for t in range(T)]
        dba_0, dba_1, dba_2, dba_3 = [dbasis_step(t) for t in range(T)]
        squ_0, squ_1, squ_2, squ_3 = [square_step(jj) for jj in range(J)]
        plain_low, plain_high = plain_step((0, 1)), plain_step((2, 3))
        o1_mm_0, o1_mm_1 = out_1_matmul_step(0), out_1_matmul_step(1)
        o1_st_0, o1_st_1 = out_1_store_step(0), out_1_store_step(1)
        take_plain, take_weighted = pair_step(take_plain_sum, 2), pair_step(take_weighted_sum, 3)
        back, store_0 = pair_step(transpose_back, 5), pair_step(store_out_0, 5)

        steady = (
            squ_0, mul_0, x_transpose_step, o1_mm_0, x_copy_step, o1_mm_1, dba_3, squ_1, weighted_step,
            weight_transpose_step, mul_1, mul_2, plain_low, squ_2, o1_st_0, back, plain_high, squ_3, o1_st_1, round_step,
            mul_3, quantise_step, take_weighted, weigh_step, weight_copy_step, store_0, dba_0, exponential_step, dba_1,
            dba_2, take_plain, weight_quantise_step,
        )
        slot_0 = (
            second_chunk_copy, dba_3, mul_0, second_half_interleave, mul_1, first_round, squ_0, second_chunk_quantise, squ_1,
            weight_transpose_step, second_half_transpose, squ_2, x_transpose_step, round_step, squ_3, dba_0, mul_2, dba_1,
            first_quantise, dba_2, weight_copy_step, mul_3, exponential_step, weigh_step, quantise_step, x_copy_step,
            second_half_quantise,
        )
        slot_1 = (
            weight_transpose_step, grad_tokens_quantise, squ_0, plain_low, x_transpose_step, plain_high, round_step, dba_3,
            mul_0, dba_0, mul_1, dba_1, weight_copy_step, squ_1, mul_2, mul_3, quantise_step, squ_2, weigh_step,
            weight_quantise_step, dba_2, squ_3, x_copy_step, exponential_step,
        )

        with tc.manual_schedule():
            nc.gpsimd.memset(one_column[:], 0.0)
            nc.scalar.dma_start(out=grid_bf[:], in_=grid.partition_broadcast(P))
            nc.scalar.activation(out=one_column[:], in_=one_column[:], func=ACT.Exp)

            nc.sync.dma_start(out=x_sb[0][:], in_=x_hbm[0])
            nc.sync.dma_start(out=grad_sb[0][:], in_=grad_hbm[0])
            load_weight(0)
            load_weight(1)
            nc.sync.dma_start(out=grad_sb[1][:], in_=grad_hbm[1])
            nc.sync.dma_start(out=x_sb[1][:], in_=x_hbm[1])
            for c in range(2, 2 * BLOCKS):
                load_weight(c)

            make_identity(nc, identity[:])
            make_identity(nc, identity_bf[:])
            nc.vector.tensor_scalar(
                out=grid_bias[:], in0=grid_bf[:], scalar1=-INV_H, scalar2=None, op0=ALU.mult
            )
            nc.vector.tensor_copy(out=grid_f[:], in_=grid_bf[:])
            nc.vector.tensor_scalar(
                out=grid_weight[:],
                in0=grid_f[:],
                scalar1=grid_f[:, REF : REF + 1],
                scalar2=-1.0,
                op0=ALU.subtract,
                op1=ALU.mult,
            )

            for key in (("g", 0), ("w", 0), ("w", 1)):
                new_paired(key)
            for jj in range(J):
                square(0, jj)
            exponential(0)
            for k in range(2):
                copy_pairs("vector", paired["g", 0][:], k, transpose_pairs(grad_sb[0], k))
            quantise_grad_features(0)
            for k in range(2):
                copy_pairs("vector", paired["w", 0][:], k, transpose_pairs(w_raw[0], k))
            second_chunk = [transpose_pairs(w_raw[1], k) for k in range(2)]
            quantise_weight(0)
            for t in range(3):
                matmul_dbasis(0, t)
            interleave_grad(0)
            for jj in range(J):
                square(1, jj)
            exponential(1)
            copy_pairs("vector", paired["w", 1][:], 0, second_chunk[0])
            banks["second chunk"] = second_chunk[1]

            for n in range(UNITS + 4):
                for step in {0: slot_0, 1: slot_1}.get(n, steady):
                    step(n)
